import numpy as np
import ml_dtypes


BF16 = ml_dtypes.bfloat16


def bf(x):
    return np.asarray(x, np.float32).astype(BF16)


def f64(x):
    return np.asarray(x).astype(np.float64)


E2M1 = np.array([0.0, 0.5, 1.0, 1.5, 2.0, 3.0, 4.0, 6.0, -0.0, -0.5, -1.0, -1.5, -2.0, -3.0, -4.0, -6.0])


def pack_weight(w, fmt):
    k, n = w.shape
    w = f64(bf(w)).reshape(k // 32, 32, n)
    amax = np.abs(w).max(1)
    if fmt == "e4m3":
        byte = np.frexp(amax)[1] - 1 + 127 - 7
    else:
        mant, ex = np.frexp(amax / 6.0)
        byte = np.where(mant > 0.5, ex, ex - 1) + 127
    byte = np.clip(np.where(amax > 0, byte, 1), 1, 254)
    scaled = (w * np.exp2(127.0 - byte)[:, None, :]).reshape(k, n).astype(np.float32)
    by_word = np.ascontiguousarray(scaled.reshape(k // 512, 128, 4, n).transpose(0, 1, 3, 2))
    if fmt == "e4m3":
        words = by_word.astype(ml_dtypes.float8_e4m3fn).view(np.uint8)
    else:
        c = by_word.astype(ml_dtypes.float4_e2m1fn).view(np.uint8) & 0xF
        words = c[..., 0::2] | (c[..., 1::2] << 4)
    return np.ascontiguousarray(words), np.ascontiguousarray(byte.astype(np.uint8).reshape(k // 512, 16, n))


def unpack_weight(words, scales, fmt):
    g, p, n, _ = words.shape
    if fmt == "e4m3":
        vals = np.ascontiguousarray(words).view(ml_dtypes.float8_e4m3fn).astype(np.float64)
    else:
        nib = np.empty((g, p, n, 4), np.uint8)
        nib[..., 0::2] = words & 0xF
        nib[..., 1::2] = words >> 4
        vals = E2M1[nib]
    vals = vals * np.repeat(np.exp2(scales.astype(np.float64) - 127.0), 8, axis=1)[..., None]
    return vals.transpose(0, 1, 3, 2).reshape(g * 512, n)

def pack4(w):
    words, scales = pack_weight(w, "e2m1")
    return words.reshape(words.shape[0], 128, -1), scales


def unpack4(words, scales):
    return unpack_weight(words.reshape(words.shape[0], 128, -1, 2), scales, "e2m1")


def kspread(k):
    return np.exp2(np.repeat(np.random.randint(-6, 7, k // 32), 32).astype(np.float64))


B, N, D, H, DH = 2, 512, 2048, 16, 64
INNER = H * DH


def dpfp(u):
    u2 = np.concatenate([np.maximum(u, 0.0), np.maximum(-u, 0.0)], axis=-1)
    return u2 * np.roll(u2, 1, axis=-1)


def heads(t):
    return t.reshape(B, N, H, DH).transpose(0, 2, 1, 3)


def setup_inputs():
    s = kspread(D)
    x = np.random.standard_normal((B, N, D)) * s
    x_words, x_scales = pack4(x.reshape(B * N, D).T)
    words, scales = pack4(np.random.standard_normal((D, 2 * INNER)) / np.sqrt(D) / s[:, None])
    return {"x_words": x_words, "x_scales": x_scales, "w_qk_words": words, "w_qk_scales": scales}


def reference(x_words, x_scales, w_qk_words, w_qk_scales):
    qk = unpack4(x_words, x_scales).T.reshape(B, N, D) @ unpack4(w_qk_words, w_qk_scales)
    q, k = np.split(qk, 2, axis=-1)
    q, k = dpfp(heads(q)), dpfp(heads(k))
    return q / q.sum(-1, keepdims=True), k / k.sum(-1, keepdims=True)

@@ -1,0 +1,196 @@
+from contextlib import ExitStack
+
+import concourse.mybir as mybir
+
+P = 128
+B, T, D, H, DH = 2, 512, 2048, 16, 64
+ROWS = B * T
+COLS = 2 * H * DH
+PASSES = D // 512
+N = 512
+HEADS = N // DH
+CHUNKS = COLS // N
+TILES = ROWS // P
+FLOPS = 2 * ROWS * D * COLS
+
+F32 = mybir.dt.float32
+I32 = mybir.dt.int32
+U8 = mybir.dt.uint8
+FP4 = mybir.dt.float4_e2m1fn_x4
+ALU = mybir.AluOpType
+ACT = mybir.ActivationFunctionType
+
+LEAD = 4
+STRETCH = LEAD + DH
+G_EVERY = 4
+
+
+def tile_dpfpattention_pa_kernel(tc, x_words, x_scales, w_words, w_scales, out_0, out_1):
+    nc = tc.nc
+    outs = (out_0, out_1)
+
+    with ExitStack() as ctx:
+        keep = ctx.enter_context(tc.tile_pool(name="keep", bufs=1))
+        work = ctx.enter_context(tc.tile_pool(name="work", bufs=4))
+        res = ctx.enter_context(tc.tile_pool(name="res", bufs=6))
+        psum = ctx.enter_context(tc.psum_pool(name="psum", bufs=8))
+        ctx.enter_context(tc.manual_schedule())
+
+        xw = []
+        for half in range(2):
+            xw_tile = keep.tile([P, PASSES, 2 * T], U8, align_bytes=64, name="xw%d" % half)
+            xw.append(xw_tile)
+        ww = []
+        for c in range(CHUNKS):
+            ww_tile = keep.tile([P, PASSES, 2 * N], U8, align_bytes=64, name="ww%d" % c)
+            ww.append(ww_tile)
+        xs = keep.tile([P, PASSES, ROWS], U8, align_bytes=64, name="xs")
+        ws_first = keep.tile([P, PASSES, N], U8, align_bytes=64, name="ws_first")
+        ws_rest = keep.tile([P, PASSES, COLS - N], U8, align_bytes=64, name="ws_rest")
+        warm = keep.tile([P, 1], F32, name="warm")
+
+        nc.vector.memset(xs[:, 0:2, :].bitcast(I32), 0)
+        nc.gpsimd.memset(xs[:, 2:4, :].bitcast(I32), 0)
+        nc.vector.memset(ws_first[:].bitcast(I32), 0)
+        nc.vector.memset(warm[:], 0.0)
+        nc.scalar.activation(out=warm[:], in_=warm[:], func=ACT.Relu)
+        nc.gpsimd.memset(ws_rest[:].bitcast(I32), 0)
+
+        def load_x(half, g0, g1):
+            nc.sync.dma_start(
+                out=xw[half][:, g0:g1, :].bitcast(I32),
+                in_=x_words[g0:g1, :, half * 2 * T : (half + 1) * 2 * T].rearrange("g p c -> p g c").bitcast(I32),
+            )
+
+        def load_w(c, g0, g1):
+            nc.sync.dma_start(
+                out=ww[c][:, g0:g1, :].bitcast(I32),
+                in_=w_words[g0:g1, :, c * 2 * N : (c + 1) * 2 * N].rearrange("g p c -> p g c").bitcast(I32),
+            )
+
+        def load_scales(planes, scales):
+            for q in range(4):
+                nc.sync.dma_start(
+                    out=planes[32 * q : 32 * q + 4, :, :].bitcast(I32),
+                    in_=scales[:, 4 * q : 4 * q + 4, :].rearrange("g r n -> r g n").bitcast(I32),
+                )
+
+        load_x(0, 0, 1)
+        load_w(0, 0, 1)
+        load_scales(xs, x_scales)
+        load_scales(ws_first, w_scales[:, :, 0:N])
+        load_x(0, 1, 4)
+        load_w(0, 1, 4)
+        load_x(1, 0, 4)
+        load_scales(ws_rest, w_scales[:, :, N:COLS])
+        for c in range(1, CHUNKS):
+            load_w(c, 0, 4)
+
+        units = [(c, t) for c in range(CHUNKS) for t in range(TILES)]
+        live = {}
+
+        def multiply(i):
+            c, t = units[i]
+            half, col = divmod(t * P, T)
+            u = psum.tile([P, N], F32, name="u")
+            if c == 0:
+                ws = ws_first
+                s0 = 0
+            else:
+                ws = ws_rest
+                s0 = (c - 1) * N
+            for g in range(PASSES):
+                nc.tensor.matmul_mx(
+                    out=u[:],
+                    lhsT=xw[half][:, g, 2 * col : 2 * (col + P)].bitcast(FP4),
+                    lhsT_scale=xs[:, g, t * P : (t + 1) * P],
+                    rhs=ww[c][:, g, :].bitcast(FP4),
+                    rhs_scale=ws[:, g, s0 : s0 + N],
+                    start=(g == 0),
+                    stop=(g == PASSES - 1),
+                )
+            live[i] = {"u": u[:].rearrange("p (h d) -> p h d", d=DH)}
+
+        def copy_u(i):
+            u = live[i]["u"]
+            us = work.tile([P, HEADS, STRETCH], F32, name="us")
+            nc.scalar.copy(out=us[:, :, LEAD:STRETCH], in_=u)
+            nc.scalar.mul(us[:, :, LEAD - 1 : LEAD], u[:, :, DH - 1 : DH], -1.0)
+            live[i]["us"] = us
+
+        def product(i):
+            v = work.tile([P, HEADS, DH], F32, name="v")
+            nc.vector.tensor_tensor(
+                out=v[:], in0=live[i]["u"], in1=live[i]["us"][:, :, LEAD - 1 : STRETCH - 1], op=ALU.mult
+            )
+            live[i]["v"] = v
+
+        def relu_sum(i):
+            v = live[i]["v"]
+            p = work.tile([P, HEADS, DH], F32, name="p")
+            s = work.tile([P, HEADS], F32, name="s")
+            for h in range(HEADS):
+                nc.scalar.activation(out=p[:, h, :], in_=v[:, h, :], func=ACT.Relu, accum_out=s[:, h : h + 1])
+            live[i]["p"] = p
+            live[i]["s"] = s
+
+        def invert(i):
+            r = work.tile([P, HEADS], F32, name="r")
+            nc.vector.reciprocal(out=r[:], in_=live[i]["s"][:])
+            live[i]["r"] = r
+
+        def normalise(i):
+            qn = work.tile([P, HEADS, DH], F32, name="qn")
+            nc.gpsimd.tensor_tensor(
+                out=qn[:],
+                in0=live[i]["p"][:],
+                in1=live[i]["r"][:].unsqueeze(2).to_broadcast([P, HEADS, DH]),
+                op=ALU.mult,
+            )
+            live[i]["qn"] = qn
+
+        def split(i):
+            u, qn = live[i]["u"], live[i]["qn"]
+            phi = res.tile([P, HEADS, 2 * DH], F32, name="phi")
+            nc.vector.scalar_tensor_tensor(
+                out=phi[:, :, 0:DH], in0=u, scalar=0.0, in1=qn[:], op0=ALU.is_gt, op1=ALU.mult
+            )
+            live[i]["phi"] = phi
+            if i % G_EVERY:
+                nc.vector.scalar_tensor_tensor(
+                    out=phi[:, :, DH : 2 * DH], in0=u, scalar=0.0, in1=qn[:], op0=ALU.is_lt, op1=ALU.mult
+                )
+
+        def rest(i):
+            qn, phi = live[i]["qn"], live[i]["phi"]
+            if i % G_EVERY == 0:
+                nc.gpsimd.tensor_tensor(
+                    out=phi[:, :, DH : 2 * DH], in0=qn[:], in1=phi[:, :, 0:DH], op=ALU.subtract
+                )
+
+        def store(i):
+            c, t = units[i]
+            which, h0 = divmod(c * HEADS, H)
+            batch, t0 = divmod(t * P, T)
+            nc.sync.dma_start(
+                out=outs[which][batch, h0 : h0 + HEADS, t0 : t0 + P, :].rearrange("h t f -> t h f"),
+                in_=live[i]["phi"][:],
+            )
+
+        n = len(units)
+        for i in range(n + 3):
+            if i < n:
+                multiply(i)
+                copy_u(i)
+                product(i)
+            if 0 <= i - 1 < n:
+                relu_sum(i - 1)
+            if 0 <= i - 3 < n:
+                split(i - 3)
+            if 0 <= i - 1 < n:
+                invert(i - 1)
+            if 0 <= i - 3 < n:
+                rest(i - 3)
+                store(i - 3)
+            if 0 <= i - 1 < n:
+                normalise(i - 1)

@@ -22,7 +22,6 @@ ACT = mybir.ActivationFunctionType
 
 LEAD = 4
 STRETCH = LEAD + DH
-G_EVERY = 4
 
 
 def tile_dpfpattention_pa_kernel(tc, x_words, x_scales, w_words, w_scales, out_0, out_1):
@@ -156,16 +155,9 @@ def tile_dpfpattention_pa_kernel(tc, x_words, x_scales, w_words, w_scales, out_0
                 out=phi[:, :, 0:DH], in0=u, scalar=0.0, in1=qn[:], op0=ALU.is_gt, op1=ALU.mult
             )
             live[i]["phi"] = phi
-            if i % G_EVERY:
+            if True:
                 nc.vector.scalar_tensor_tensor(
                     out=phi[:, :, DH : 2 * DH], in0=u, scalar=0.0, in1=qn[:], op0=ALU.is_lt, op1=ALU.mult
-                )
-
-        def rest(i):
-            qn, phi = live[i]["qn"], live[i]["phi"]
-            if i % G_EVERY == 0:
-                nc.gpsimd.tensor_tensor(
-                    out=phi[:, :, DH : 2 * DH], in0=qn[:], in1=phi[:, :, 0:DH], op=ALU.subtract
                 )
 
         def store(i):
@@ -190,7 +182,6 @@ def tile_dpfpattention_pa_kernel(tc, x_words, x_scales, w_words, w_scales, out_0
             if 0 <= i - 1 < n:
                 invert(i - 1)
             if 0 <= i - 3 < n:
-                rest(i - 3)
                 store(i - 3)
             if 0 <= i - 1 < n:
                 normalise(i - 1)

from contextlib import ExitStack

import concourse.mybir as mybir

P = 128
B, T, D, H, DH = 2, 512, 2048, 16, 64
ROWS = B * T
COLS = 2 * H * DH
PASSES = D // 512
N = 512
HEADS = N // DH
CHUNKS = COLS // N
TILES = ROWS // P
FLOPS = 2 * ROWS * D * COLS

F32 = mybir.dt.float32
I32 = mybir.dt.int32
U8 = mybir.dt.uint8
FP4 = mybir.dt.float4_e2m1fn_x4
ALU = mybir.AluOpType
ACT = mybir.ActivationFunctionType

LEAD = 4
STRETCH = LEAD + DH


def tile_dpfpattention_pa_kernel(tc, x_words, x_scales, w_words, w_scales, out_0, out_1):
    nc = tc.nc
    outs = (out_0, out_1)

    with ExitStack() as ctx:
        keep = ctx.enter_context(tc.tile_pool(name="keep", bufs=1))
        work = ctx.enter_context(tc.tile_pool(name="work", bufs=4))
        res = ctx.enter_context(tc.tile_pool(name="res", bufs=6))
        psum = ctx.enter_context(tc.psum_pool(name="psum", bufs=8))
        ctx.enter_context(tc.manual_schedule())

        xw = []
        for half in range(2):
            xw_tile = keep.tile([P, PASSES, 2 * T], U8, align_bytes=64, name="xw%d" % half)
            xw.append(xw_tile)
        ww = []
        for c in range(CHUNKS):
            ww_tile = keep.tile([P, PASSES, 2 * N], U8, align_bytes=64, name="ww%d" % c)
            ww.append(ww_tile)
        xs = keep.tile([P, PASSES, ROWS], U8, align_bytes=64, name="xs")
        ws_first = keep.tile([P, PASSES, N], U8, align_bytes=64, name="ws_first")
        ws_rest = keep.tile([P, PASSES, COLS - N], U8, align_bytes=64, name="ws_rest")
        warm = keep.tile([P, 1], F32, name="warm")

        nc.vector.memset(xs[:, 0:2, :].bitcast(I32), 0)
        nc.gpsimd.memset(xs[:, 2:4, :].bitcast(I32), 0)
        nc.vector.memset(ws_first[:].bitcast(I32), 0)
        nc.vector.memset(warm[:], 0.0)
        nc.scalar.activation(out=warm[:], in_=warm[:], func=ACT.Relu)
        nc.gpsimd.memset(ws_rest[:].bitcast(I32), 0)

        def load_x(half, g0, g1):
            nc.sync.dma_start(
                out=xw[half][:, g0:g1, :].bitcast(I32),
                in_=x_words[g0:g1, :, half * 2 * T : (half + 1) * 2 * T].rearrange("g p c -> p g c").bitcast(I32),
            )

        def load_w(c, g0, g1):
            nc.sync.dma_start(
                out=ww[c][:, g0:g1, :].bitcast(I32),
                in_=w_words[g0:g1, :, c * 2 * N : (c + 1) * 2 * N].rearrange("g p c -> p g c").bitcast(I32),
            )

        def load_scales(planes, scales):
            for q in range(4):
                nc.sync.dma_start(
                    out=planes[32 * q : 32 * q + 4, :, :].bitcast(I32),
                    in_=scales[:, 4 * q : 4 * q + 4, :].rearrange("g r n -> r g n").bitcast(I32),
                )

        load_x(0, 0, 1)
        load_w(0, 0, 1)
        load_scales(xs, x_scales)
        load_scales(ws_first, w_scales[:, :, 0:N])
        load_x(0, 1, 4)
        load_w(0, 1, 4)
        load_x(1, 0, 4)
        load_scales(ws_rest, w_scales[:, :, N:COLS])
        for c in range(1, CHUNKS):
            load_w(c, 0, 4)

        units = [(c, t) for c in range(CHUNKS) for t in range(TILES)]
        live = {}

        def multiply(i):
            c, t = units[i]
            half, col = divmod(t * P, T)
            u = psum.tile([P, N], F32, name="u")
            if c == 0:
                ws = ws_first
                s0 = 0
            else:
                ws = ws_rest
                s0 = (c - 1) * N
            for g in range(PASSES):
                nc.tensor.matmul_mx(
                    out=u[:],
                    lhsT=xw[half][:, g, 2 * col : 2 * (col + P)].bitcast(FP4),
                    lhsT_scale=xs[:, g, t * P : (t + 1) * P],
                    rhs=ww[c][:, g, :].bitcast(FP4),
                    rhs_scale=ws[:, g, s0 : s0 + N],
                    start=(g == 0),
                    stop=(g == PASSES - 1),
                )
            live[i] = {"u": u[:].rearrange("p (h d) -> p h d", d=DH)}

        def copy_u(i):
            u = live[i]["u"]
            us = work.tile([P, HEADS, STRETCH], F32, name="us")
            nc.scalar.copy(out=us[:, :, LEAD:STRETCH], in_=u)
            nc.scalar.mul(us[:, :, LEAD - 1 : LEAD], u[:, :, DH - 1 : DH], -1.0)
            live[i]["us"] = us

        def product(i):
            v = work.tile([P, HEADS, DH], F32, name="v")
            nc.vector.tensor_tensor(
                out=v[:], in0=live[i]["u"], in1=live[i]["us"][:, :, LEAD - 1 : STRETCH - 1], op=ALU.mult
            )
            live[i]["v"] = v

        def relu_sum(i):
            v = live[i]["v"]
            p = work.tile([P, HEADS, DH], F32, name="p")
            s = work.tile([P, HEADS], F32, name="s")
            for h in range(HEADS):
                nc.scalar.activation(out=p[:, h, :], in_=v[:, h, :], func=ACT.Relu, accum_out=s[:, h : h + 1])
            live[i]["p"] = p
            live[i]["s"] = s

        def invert(i):
            r = work.tile([P, HEADS], F32, name="r")
            nc.vector.reciprocal(out=r[:], in_=live[i]["s"][:])
            live[i]["r"] = r

        def normalise(i):
            qn = work.tile([P, HEADS, DH], F32, name="qn")
            nc.gpsimd.tensor_tensor(
                out=qn[:],
                in0=live[i]["p"][:],
                in1=live[i]["r"][:].unsqueeze(2).to_broadcast([P, HEADS, DH]),
                op=ALU.mult,
            )
            live[i]["qn"] = qn

        def split(i):
            u, qn = live[i]["u"], live[i]["qn"]
            phi = res.tile([P, HEADS, 2 * DH], F32, name="phi")
            nc.vector.scalar_tensor_tensor(
                out=phi[:, :, 0:DH], in0=u, scalar=0.0, in1=qn[:], op0=ALU.is_gt, op1=ALU.mult
            )
            live[i]["phi"] = phi
            if True:
                nc.vector.scalar_tensor_tensor(
                    out=phi[:, :, DH : 2 * DH], in0=u, scalar=0.0, in1=qn[:], op0=ALU.is_lt, op1=ALU.mult
                )

        def store(i):
            c, t = units[i]
            which, h0 = divmod(c * HEADS, H)
            batch, t0 = divmod(t * P, T)
            nc.sync.dma_start(
                out=outs[which][batch, h0 : h0 + HEADS, t0 : t0 + P, :].rearrange("h t f -> t h f"),
                in_=live[i]["phi"][:],
            )

        n = len(units)
        for i in range(n + 3):
            if i < n:
                multiply(i)
                copy_u(i)
                product(i)
            if 0 <= i - 1 < n:
                relu_sum(i - 1)
            if 0 <= i - 3 < n:
                split(i - 3)
            if 0 <= i - 1 < n:
                invert(i - 1)
            if 0 <= i - 3 < n:
                store(i - 3)
            if 0 <= i - 1 < n:
                normalise(i - 1)
